import numpy as np
import ml_dtypes


def mxq(x, axis, fmt="e4m3"):
    dtype, down = {"e4m3": (ml_dtypes.float8_e4m3fn, 7), "e5m2": (ml_dtypes.float8_e5m2, 14)}[fmt]
    v = np.moveaxis(np.asarray(x, np.float32).astype(ml_dtypes.bfloat16).astype(np.float64), axis, -1)
    blocks = v.reshape(v.shape[:-1] + (-1, 32))
    amax = np.abs(blocks).max(-1, keepdims=True)
    byte = np.maximum(np.where(amax > 0, np.frexp(amax)[1] - 1 + 127, 0) - down, 1)
    scale = np.exp2(byte - 127.0)
    codes = (blocks / scale).astype(np.float32).astype(dtype).astype(np.float64)
    return np.moveaxis((codes * scale).reshape(v.shape), -1, axis)


WIDE = False


def mx_kscale(k):
    if not WIDE:
        return np.ones(k)
    levels = np.array([10, -10, 5, -5, 0])
    if k % 512:
        return np.exp2(np.random.permutation(np.resize(levels, k // 32))).repeat(32)
    a = np.empty((k // 512, 16))
    for p in range(k // 512):
        a[p, :8] = np.random.permutation(np.resize(levels, 8))
        for g in range(8):
            far = levels[np.abs(levels - a[p, g]) >= 10]
            a[p, g + 8] = far[np.random.randint(len(far))]
    return np.exp2(a.ravel()).repeat(32)


BF16 = ml_dtypes.bfloat16


def bf(x):
    return np.asarray(x, np.float32).astype(BF16)


def f64(x):
    return np.asarray(x).astype(np.float64)


E2M1 = np.array([0.0, 0.5, 1.0, 1.5, 2.0, 3.0, 4.0, 6.0, -0.0, -0.5, -1.0, -1.5, -2.0, -3.0, -4.0, -6.0])


def pack_weight(w, fmt):
    k, n = w.shape
    w = f64(bf(w)).reshape(k // 32, 32, n)
    amax = np.abs(w).max(1)
    if fmt == "e4m3":
        byte = np.frexp(amax)[1] - 1 + 127 - 7
    else:
        mant, ex = np.frexp(amax / 6.0)
        byte = np.where(mant > 0.5, ex, ex - 1) + 127
    byte = np.clip(np.where(amax > 0, byte, 1), 1, 254)
    scaled = (w * np.exp2(127.0 - byte)[:, None, :]).reshape(k, n).astype(np.float32)
    by_word = np.ascontiguousarray(scaled.reshape(k // 512, 128, 4, n).transpose(0, 1, 3, 2))
    if fmt == "e4m3":
        words = by_word.astype(ml_dtypes.float8_e4m3fn).view(np.uint8)
    else:
        c = by_word.astype(ml_dtypes.float4_e2m1fn).view(np.uint8) & 0xF
        words = c[..., 0::2] | (c[..., 1::2] << 4)
    return np.ascontiguousarray(words), np.ascontiguousarray(byte.astype(np.uint8).reshape(k // 512, 16, n))


def unpack_weight(words, scales, fmt):
    g, p, n, _ = words.shape
    if fmt == "e4m3":
        vals = np.ascontiguousarray(words).view(ml_dtypes.float8_e4m3fn).astype(np.float64)
    else:
        nib = np.empty((g, p, n, 4), np.uint8)
        nib[..., 0::2] = words & 0xF
        nib[..., 1::2] = words >> 4
        vals = E2M1[nib]
    vals = vals * np.repeat(np.exp2(scales.astype(np.float64) - 127.0), 8, axis=1)[..., None]
    return vals.transpose(0, 1, 3, 2).reshape(g * 512, n)


B, I, H, ORDER = 8192, 512, 256, 2
OH = ORDER * H


def sigmoid(v):
    return 1.0 / (1.0 + np.exp(-v))


def draw0():
    s, t = mx_kscale(I), mx_kscale(OH)
    x = bf(np.random.standard_normal((B, I)) * s)
    me_output = bf(np.random.standard_normal((B, OH)) * t)
    W_memi_words, W_memi_scales = pack_weight(np.random.standard_normal((I, OH)) * 0.7 / np.sqrt(I) / s[:, None], "e4m3")
    W_memh_words, W_memh_scales = pack_weight(np.random.standard_normal((OH, OH)) * 0.7 / np.sqrt(OH) / t[:, None], "e4m3")
    W_memt_words, W_memt_scales = pack_weight(np.random.standard_normal((OH, H)) * 1.0 / np.sqrt(OH) / t[:, None], "e4m3")
    return {"x": x,
            "me_output": me_output,
            "W_memi_words": W_memi_words,
            "W_memi_scales": W_memi_scales,
            "W_memh_words": W_memh_words,
            "W_memh_scales": W_memh_scales,
            "W_memt_words": W_memt_words,
            "W_memt_scales": W_memt_scales,
            "mem_bias": bf(np.random.standard_normal(OH) * 0.3)}


def core(x, me_output, W_memi_words, W_memi_scales, W_memh_words, W_memh_scales, W_memt_words, W_memt_scales, mem_bias):
    me = f64(me_output)
    mg = ((mxq(f64(x), 1, "e4m3") @ unpack_weight(W_memi_words, W_memi_scales, "e4m3"))
          + (mxq(me, 1, "e4m3") @ unpack_weight(W_memh_words, W_memh_scales, "e4m3"))
          + f64(mem_bias))
    gated = sigmoid(mg) * me
    return mxq(gated, 1, "e4m3") @ unpack_weight(W_memt_words, W_memt_scales, "e4m3")


def e4m3fn_bytes(y):
    return np.clip(np.asarray(y, np.float64), -448.0, 448.0).astype(np.float32).astype(ml_dtypes.float8_e4m3fn).view(np.uint8)


def e4m3fn_values(b):
    return np.asarray(b, np.uint8).view(ml_dtypes.float8_e4m3fn).astype(np.float64)


def setup_inputs():
    d = draw0()
    x0 = np.asarray(d['x']).astype(np.float64)
    s = (np.max(np.abs(x0), axis=(0,), keepdims=True) / 448.0).astype(np.float32)
    out = {}
    for k, v in d.items():
        if k == 'x':
            out['x_bytes'] = e4m3fn_bytes(x0 / s.astype(np.float64))
            out['x_scale'] = s
        else:
            out[k] = v
    return out


def reference(x_bytes, x_scale, me_output, W_memi_words, W_memi_scales, W_memh_words, W_memh_scales, W_memt_words, W_memt_scales, mem_bias):
    return core(e4m3fn_values(x_bytes) * x_scale.astype(np.float64), me_output, W_memi_words, W_memi_scales, W_memh_words, W_memh_scales, W_memt_words, W_memt_scales, mem_bias)

@@ -1,0 +1,243 @@
+from contextlib import ExitStack
+
+import concourse.mybir as mybir
+from concourse.masks import make_identity
+
+TOKENS, K, CH, N_OUT = 8192, 512, 512, 256
+FLOPS = 2 * TOKENS * (K * CH + CH * CH + CH * N_OUT)
+
+F32 = mybir.dt.float32
+BF16 = mybir.dt.bfloat16
+I32 = mybir.dt.int32
+U32 = mybir.dt.uint32
+U8 = mybir.dt.uint8
+FP8 = mybir.dt.float8_e4m3fn
+FP8X4 = mybir.dt.float8_e4m3fn_x4
+MULT = mybir.AluOpType.mult
+ACT = mybir.ActivationFunctionType
+
+P = 128
+PACK = 4
+TILES = TOKENS // P
+G = 4
+GROUPS = TILES // G
+GT = G * P
+AHEAD = 4
+
+
+def tile_lstmcell_pa_t_w8_kernel(
+    tc, x_bytes, x_scale, me_output, wi_words, wi_scales, wh_words, wh_scales, wt_words, wt_scales, mem_bias, out
+):
+    nc = tc.nc
+    x_hbm = x_bytes.rearrange("(p i) k -> p i k", i=TILES)
+    me_hbm = me_output.rearrange("(p i) k -> p i k", i=TILES)
+    out_hbm = out.rearrange("(p i) n -> p i n", i=TILES)
+
+    with ExitStack() as ctx:
+        keep = ctx.enter_context(tc.tile_pool(name="keep", bufs=1))
+        xin = ctx.enter_context(tc.tile_pool(name="xin", bufs=6))
+        mein = ctx.enter_context(tc.tile_pool(name="mein", bufs=7))
+        work = ctx.enter_context(tc.tile_pool(name="work", bufs=3))
+        megp = ctx.enter_context(tc.tile_pool(name="megp", bufs=5))
+        outp = ctx.enter_context(tc.tile_pool(name="outp", bufs=3))
+        ptp = ctx.enter_context(tc.psum_pool(name="ptp", bufs=3))
+        pmg = ctx.enter_context(tc.psum_pool(name="pmg", bufs=3))
+        pout = ctx.enter_context(tc.psum_pool(name="pout", bufs=2))
+        ctx.enter_context(tc.manual_schedule())
+
+        ident = keep.tile([P, P], F32, name="ident")
+        s_col = keep.tile([P, PACK], F32, name="s_col")
+        scale = keep.tile([P, G * K], F32, name="scale")
+        bias_bf = keep.tile([P, PACK], BF16, name="bias_bf")
+        bias = keep.tile([P, PACK], F32, name="bias")
+        warm = keep.tile([P, 1], F32, name="warm")
+        wi_raw = keep.tile([P, CH], U32, name="wi_raw", align_bytes=64)
+        wh_raw = keep.tile([P, CH], U32, name="wh_raw", align_bytes=64)
+        wi = keep.tile([P, CH], U32, name="wi", align_bytes=64)
+        wh = keep.tile([P, CH], U32, name="wh", align_bytes=64)
+        wt = keep.tile([P, N_OUT], U32, name="wt", align_bytes=64)
+        ws_raw = keep.tile([P, 2 * CH], U8, name="ws_raw", align_bytes=64)
+        ws = keep.tile([P, 2 * CH], U8, name="ws", align_bytes=64)
+        wts = keep.tile([P, N_OUT], U8, name="wts", align_bytes=64)
+
+        xb, me, xw, xg, meg = {}, {}, {}, {}, {}
+        xq, mq, sig, gated, gq, res = {}, {}, {}, {}, {}, {}
+
+        def load_x(g):
+            t = xin.tile([P, G, K], U8, name="xb")
+            nc.sync.dma_start(out=t[:], in_=x_hbm[:, g * G : (g + 1) * G, :])
+            xb[g] = t
+
+        def load_me(g):
+            t = mein.tile([P, G, K], BF16, name="me")
+            nc.sync.dma_start(out=t[:], in_=me_hbm[:, g * G : (g + 1) * G, :])
+            me[g] = t
+
+        def load(g):
+            load_x(g)
+            load_me(g)
+
+        def widen(g):
+            t = work.tile([P, G * K], BF16, name="xw")
+            src = xb[g][:].rearrange("p i k -> p (i k)")
+            pieces = G if g == 0 else 1
+            w = G * K // pieces
+            for j in range(pieces):
+                nc.vector.tensor_tensor(
+                    out=t[:, j * w : (j + 1) * w],
+                    in0=src[:, j * w : (j + 1) * w].bitcast(FP8),
+                    in1=scale[:, 0:w],
+                    op=MULT,
+                )
+            xw[g] = t
+
+        def turn(src, dst):
+            words = src.bitcast(F32)
+            dst_w = dst.bitcast(F32).rearrange("p (i r u) -> p i r u", i=G, u=2)
+            for b in range(G // 2):
+                pt = ptp.tile([P, 2, 2, P], F32, name="pt")
+                for i in range(2):
+                    for u in range(2):
+                        base = (2 * b + i) * (K // 2)
+                        nc.tensor.transpose(pt[:, i, u, :], words[:, base + u : base + K // 2 : 2], ident[:])
+                nc.scalar.copy(out=dst_w[:, 2 * b : 2 * b + 2], in_=pt[:].rearrange("p i u r -> p i r u"))
+
+        def transposes(g):
+            mg_t = megp.tile([P, GT * PACK], BF16, name="meg", align_bytes=64)
+            turn(me[g][:].rearrange("p i k -> p (i k)"), mg_t[:])
+            meg[g] = mg_t
+            xg_t = work.tile([P, GT * PACK], BF16, name="xg", align_bytes=64)
+            turn(xw[g][:], xg_t[:])
+            xg[g] = xg_t
+
+        def quant(src, cname, sname):
+            codes = work.tile([P, GT], U32, name=cname, align_bytes=64)
+            scales = work.tile([P, GT], U8, name=sname, align_bytes=64)
+            nc.vector.quantize_mx(out=codes[:].bitcast(FP8X4), scales=scales[:], in_=src)
+            return codes, scales
+
+        def gates(g):
+            s = work.tile([P, PACK, GT], F32, name="sig")
+            for t in range(PACK):
+                cols = slice(t * P, (t + 1) * P)
+                pm = pmg.tile([P, GT], F32, name="pm")
+                nc.tensor.matmul_mx(
+                    out=pm[:], lhsT=wi[:, cols].bitcast(FP8X4), lhsT_scale=ws[:, t * P : (t + 1) * P],
+                    rhs=xq[g][0][:].bitcast(FP8X4), rhs_scale=xq[g][1][:], start=True, stop=False,
+                )
+                nc.tensor.matmul_mx(
+                    out=pm[:], lhsT=wh[:, cols].bitcast(FP8X4), lhsT_scale=ws[:, CH + t * P : CH + (t + 1) * P],
+                    rhs=mq[g][0][:].bitcast(FP8X4), rhs_scale=mq[g][1][:], start=False, stop=True,
+                )
+                nc.scalar.activation(out=s[:, t, :], in_=pm[:], func=ACT.Sigmoid, bias=bias[:, t : t + 1])
+            sig[g] = s
+
+        def pieces_of(g):
+            return 2 if g == GROUPS - 1 else 1
+
+        def gate(g):
+            t = work.tile([P, GT * PACK], BF16, name="gated", align_bytes=64)
+            n = GT // pieces_of(g)
+            for j in range(pieces_of(g)):
+                cols = slice(j * n * PACK, (j + 1) * n * PACK)
+                nc.vector.tensor_tensor(
+                    out=t[:, cols].rearrange("p (r t) -> p r t", t=PACK),
+                    in0=sig[g][:, :, j * n : (j + 1) * n].rearrange("p t r -> p r t"),
+                    in1=meg[g][:, cols].rearrange("p (r t) -> p r t", t=PACK),
+                    op=MULT,
+                )
+            gated[g] = t
+
+        def quant_gated(g):
+            codes = work.tile([P, GT], U32, name="gc", align_bytes=64)
+            scales = work.tile([P, GT], U8, name="gs", align_bytes=64)
+            n = GT // pieces_of(g)
+            for j in range(pieces_of(g)):
+                nc.vector.quantize_mx(
+                    out=codes[:, j * n : (j + 1) * n].bitcast(FP8X4),
+                    scales=scales[:, j * n : (j + 1) * n],
+                    in_=gated[g][:, j * n * PACK : (j + 1) * n * PACK],
+                )
+            gq[g] = (codes, scales)
+
+        def read_out(g):
+            o = outp.tile([P, G, N_OUT], F32, name="res")
+            for b in range(G // 2):
+                po = pout.tile([P, 2, N_OUT], F32, name="po")
+                for i in range(2):
+                    cols = slice((2 * b + i) * P, (2 * b + i + 1) * P)
+                    nc.tensor.matmul_mx(
+                        out=po[:, i, :], lhsT=gq[g][0][:, cols].bitcast(FP8X4), lhsT_scale=gq[g][1][:, cols],
+                        rhs=wt[:].bitcast(FP8X4), rhs_scale=wts[:], start=True, stop=True,
+                    )
+                nc.scalar.copy(out=o[:, 2 * b : 2 * b + 2, :], in_=po[:])
+                if pieces_of(g) == 2:
+                    nc.sync.dma_start(
+                        out=out_hbm[:, g * G + 2 * b : g * G + 2 * b + 2, :], in_=o[:, 2 * b : 2 * b + 2, :]
+                    )
+            if pieces_of(g) == 1:
+                nc.sync.dma_start(out=out_hbm[:, g * G : (g + 1) * G, :], in_=o[:])
+
+        make_identity(nc, ident[:])
+        nc.gpsimd.memset(ws_raw[:].bitcast(I32), 0)
+        nc.gpsimd.memset(wts[:].bitcast(I32), 0)
+        nc.gpsimd.memset(warm[:], 0.0)
+        nc.scalar.activation(out=warm[:], in_=warm[:], func=ACT.Sigmoid)
+
+        nc.sync.dma_start(out=s_col[:], in_=x_scale.rearrange("o (p t) -> p (o t)", t=PACK))
+        nc.sync.dma_start(out=wi_raw[:].bitcast(I32), in_=wi_words[0].rearrange("p n t -> p (n t)").bitcast(I32))
+        nc.sync.dma_start(out=wh_raw[:].bitcast(I32), in_=wh_words[0].rearrange("p n t -> p (n t)").bitcast(I32))
+        load(0)
+        load(1)
+        nc.sync.dma_start(out=bias_bf[:], in_=mem_bias.rearrange("(p t) -> p t", t=PACK))
+        nc.sync.dma_start(out=wt[:].bitcast(I32), in_=wt_words[0].rearrange("p n t -> p (n t)").bitcast(I32))
+        for q in range(4):
+            for w, hbm in enumerate((wi_scales, wh_scales)):
+                nc.sync.dma_start(
+                    out=ws_raw[32 * q : 32 * q + 4, w * CH : (w + 1) * CH].bitcast(I32),
+                    in_=hbm[0, 4 * q : 4 * q + 4, :].bitcast(I32),
+                )
+            nc.sync.dma_start(
+                out=wts[32 * q : 32 * q + 4, :].bitcast(I32), in_=wt_scales[0, 4 * q : 4 * q + 4, :].bitcast(I32)
+            )
+        for g in range(2, AHEAD):
+            load(g)
+
+        ps = ptp.tile([P, PACK, P], F32, name="pt")
+        for t in range(PACK):
+            nc.tensor.transpose(ps[:, t, :], s_col[:, t : t + 1].to_broadcast([P, P]), ident[:])
+        for j in range(G):
+            nc.scalar.copy(
+                out=scale[:, j * K : (j + 1) * K].rearrange("p (n t) -> p n t", t=PACK),
+                in_=ps[:].rearrange("p t n -> p n t"),
+            )
+        nc.scalar.copy(out=bias[:], in_=bias_bf[:])
+        for raw, dst in ((wi_raw, wi), (wh_raw, wh)):
+            nc.vector.tensor_copy(
+                out=dst[:].bitcast(I32).rearrange("p (t m) -> p t m", t=PACK),
+                in_=raw[:].bitcast(I32).rearrange("p (m t) -> p t m", t=PACK),
+            )
+
+        for s in range(GROUPS + 5):
+            if s + AHEAD < GROUPS:
+                load(s + AHEAD)
+            if 0 <= s - 2 < GROUPS:
+                mq[s - 2] = quant(meg[s - 2][:], "mc", "ms")
+                xq[s - 2] = quant(xg[s - 2][:], "xc", "xs")
+            if s == 2:
+                nc.vector.tensor_copy(
+                    out=ws[:].rearrange("p (w t m) -> p w t m", w=2, t=PACK),
+                    in_=ws_raw[:].rearrange("p (w m t) -> p w t m", w=2, t=PACK),
+                )
+            if 0 <= s - 4 < GROUPS:
+                gate(s - 4)
+            if 0 <= s - 3 < GROUPS:
+                gates(s - 3)
+            if 0 <= s - 1 < GROUPS:
+                transposes(s - 1)
+            if s < GROUPS:
+                widen(s)
+            if 0 <= s - 4 < GROUPS:
+                quant_gated(s - 4)
+            if 0 <= s - 5 < GROUPS:
+                read_out(s - 5)

@@ -38,7 +38,7 @@ def tile_lstmcell_pa_t_w8_kernel(
         xin = ctx.enter_context(tc.tile_pool(name="xin", bufs=6))
         mein = ctx.enter_context(tc.tile_pool(name="mein", bufs=7))
         work = ctx.enter_context(tc.tile_pool(name="work", bufs=3))
-        megp = ctx.enter_context(tc.tile_pool(name="megp", bufs=5))
+        turnp = ctx.enter_context(tc.tile_pool(name="turnp", bufs=5))
         outp = ctx.enter_context(tc.tile_pool(name="outp", bufs=3))
         ptp = ctx.enter_context(tc.psum_pool(name="ptp", bufs=3))
         pmg = ctx.enter_context(tc.psum_pool(name="pmg", bufs=3))
@@ -60,8 +60,8 @@ def tile_lstmcell_pa_t_w8_kernel(
         ws = keep.tile([P, 2 * CH], U8, name="ws", align_bytes=64)
         wts = keep.tile([P, N_OUT], U8, name="wts", align_bytes=64)
 
-        xb, me, xw, xg, meg = {}, {}, {}, {}, {}
-        xq, mq, sig, gated, gq, res = {}, {}, {}, {}, {}, {}
+        xb, me, xw, turned, q = {}, {}, {}, {}, {}
+        sig, gated, gq = {}, {}, {}
 
         def load_x(g):
             t = xin.tile([P, G, K], U8, name="xb")
@@ -103,18 +103,16 @@ def tile_lstmcell_pa_t_w8_kernel(
                 nc.scalar.copy(out=dst_w[:, 2 * b : 2 * b + 2], in_=pt[:].rearrange("p i u r -> p i r u"))
 
         def transposes(g):
-            mg_t = megp.tile([P, GT * PACK], BF16, name="meg", align_bytes=64)
-            turn(me[g][:].rearrange("p i k -> p (i k)"), mg_t[:])
-            meg[g] = mg_t
-            xg_t = work.tile([P, GT * PACK], BF16, name="xg", align_bytes=64)
-            turn(xw[g][:], xg_t[:])
-            xg[g] = xg_t
+            t = turnp.tile([P, 2 * GT * PACK], BF16, name="turned", align_bytes=64)
+            turn(me[g][:].rearrange("p i k -> p (i k)"), t[:, 0 : GT * PACK])
+            turn(xw[g][:], t[:, GT * PACK : 2 * GT * PACK])
+            turned[g] = t
 
-        def quant(src, cname, sname):
-            codes = work.tile([P, GT], U32, name=cname, align_bytes=64)
-            scales = work.tile([P, GT], U8, name=sname, align_bytes=64)
-            nc.vector.quantize_mx(out=codes[:].bitcast(FP8X4), scales=scales[:], in_=src)
-            return codes, scales
+        def quant_in(g):
+            codes = work.tile([P, 2 * GT], U32, name="qc", align_bytes=64)
+            scales = work.tile([P, 2 * GT], U8, name="qs", align_bytes=64)
+            nc.vector.quantize_mx(out=codes[:].bitcast(FP8X4), scales=scales[:], in_=turned[g][:])
+            q[g] = (codes, scales)
 
         def gates(g):
             s = work.tile([P, PACK, GT], F32, name="sig")
@@ -123,27 +121,27 @@ def tile_lstmcell_pa_t_w8_kernel(
                 pm = pmg.tile([P, GT], F32, name="pm")
                 nc.tensor.matmul_mx(
                     out=pm[:], lhsT=wi[:, cols].bitcast(FP8X4), lhsT_scale=ws[:, t * P : (t + 1) * P],
-                    rhs=xq[g][0][:].bitcast(FP8X4), rhs_scale=xq[g][1][:], start=True, stop=False,
+                    rhs=q[g][0][:, GT:].bitcast(FP8X4), rhs_scale=q[g][1][:, GT:], start=True, stop=False,
                 )
                 nc.tensor.matmul_mx(
                     out=pm[:], lhsT=wh[:, cols].bitcast(FP8X4), lhsT_scale=ws[:, CH + t * P : CH + (t + 1) * P],
-                    rhs=mq[g][0][:].bitcast(FP8X4), rhs_scale=mq[g][1][:], start=False, stop=True,
+                    rhs=q[g][0][:, 0:GT].bitcast(FP8X4), rhs_scale=q[g][1][:, 0:GT], start=False, stop=True,
                 )
                 nc.scalar.activation(out=s[:, t, :], in_=pm[:], func=ACT.Sigmoid, bias=bias[:, t : t + 1])
             sig[g] = s
 
         def pieces_of(g):
-            return 2 if g == GROUPS - 1 else 1
+            return ((0, 2), (2, 3), (3, 4)) if g == GROUPS - 1 else ((0, G),)
 
         def gate(g):
             t = work.tile([P, GT * PACK], BF16, name="gated", align_bytes=64)
-            n = GT // pieces_of(g)
-            for j in range(pieces_of(g)):
-                cols = slice(j * n * PACK, (j + 1) * n * PACK)
+            for i0, i1 in pieces_of(g):
+                rows = slice(i0 * P, i1 * P)
+                cols = slice(i0 * P * PACK, i1 * P * PACK)
                 nc.vector.tensor_tensor(
-                    out=t[:, cols].rearrange("p (r t) -> p r t", t=PACK),
-                    in0=sig[g][:, :, j * n : (j + 1) * n].rearrange("p t r -> p r t"),
-                    in1=meg[g][:, cols].rearrange("p (r t) -> p r t", t=PACK),
+                    out=t[:, cols].rearrange("p (c i t) -> p c t i", i=4, t=PACK),
+                    in0=sig[g][:, :, rows].rearrange("p t (c i) -> p c t i", i=4),
+                    in1=turned[g][:, cols].rearrange("p (c i t) -> p c t i", i=4, t=PACK),
                     op=MULT,
                 )
             gated[g] = t
@@ -151,32 +149,29 @@ def tile_lstmcell_pa_t_w8_kernel(
         def quant_gated(g):
             codes = work.tile([P, GT], U32, name="gc", align_bytes=64)
             scales = work.tile([P, GT], U8, name="gs", align_bytes=64)
-            n = GT // pieces_of(g)
-            for j in range(pieces_of(g)):
+            for i0, i1 in pieces_of(g):
+                rows = slice(i0 * P, i1 * P)
                 nc.vector.quantize_mx(
-                    out=codes[:, j * n : (j + 1) * n].bitcast(FP8X4),
-                    scales=scales[:, j * n : (j + 1) * n],
-                    in_=gated[g][:, j * n * PACK : (j + 1) * n * PACK],
+                    out=codes[:, rows].bitcast(FP8X4),
+                    scales=scales[:, rows],
+                    in_=gated[g][:, i0 * P * PACK : i1 * P * PACK],
                 )
             gq[g] = (codes, scales)
 
         def read_out(g):
             o = outp.tile([P, G, N_OUT], F32, name="res")
-            for b in range(G // 2):
-                po = pout.tile([P, 2, N_OUT], F32, name="po")
-                for i in range(2):
-                    cols = slice((2 * b + i) * P, (2 * b + i + 1) * P)
-                    nc.tensor.matmul_mx(
-                        out=po[:, i, :], lhsT=gq[g][0][:, cols].bitcast(FP8X4), lhsT_scale=gq[g][1][:, cols],
-                        rhs=wt[:].bitcast(FP8X4), rhs_scale=wts[:], start=True, stop=True,
-                    )
-                nc.scalar.copy(out=o[:, 2 * b : 2 * b + 2, :], in_=po[:])
-                if pieces_of(g) == 2:
-                    nc.sync.dma_start(
-                        out=out_hbm[:, g * G + 2 * b : g * G + 2 * b + 2, :], in_=o[:, 2 * b : 2 * b + 2, :]
-                    )
-            if pieces_of(g) == 1:
-                nc.sync.dma_start(out=out_hbm[:, g * G : (g + 1) * G, :], in_=o[:])
+            for i0, i1 in pieces_of(g):
+                for b in range(i0, i1, 2):
+                    e = min(b + 2, i1)
+                    po = pout.tile([P, 2, N_OUT], F32, name="po")
+                    for i in range(b, e):
+                        cols = slice(i * P, (i + 1) * P)
+                        nc.tensor.matmul_mx(
+                            out=po[:, i - b, :], lhsT=gq[g][0][:, cols].bitcast(FP8X4), lhsT_scale=gq[g][1][:, cols],
+                            rhs=wt[:].bitcast(FP8X4), rhs_scale=wts[:], start=True, stop=True,
+                        )
+                    nc.scalar.copy(out=o[:, b:e, :], in_=po[:, 0 : e - b, :])
+                nc.sync.dma_start(out=out_hbm[:, g * G + i0 : g * G + i1, :], in_=o[:, i0:i1, :])
 
         make_identity(nc, ident[:])
         nc.gpsimd.memset(ws_raw[:].bitcast(I32), 0)
@@ -191,14 +186,14 @@ def tile_lstmcell_pa_t_w8_kernel(
         load(1)
         nc.sync.dma_start(out=bias_bf[:], in_=mem_bias.rearrange("(p t) -> p t", t=PACK))
         nc.sync.dma_start(out=wt[:].bitcast(I32), in_=wt_words[0].rearrange("p n t -> p (n t)").bitcast(I32))
-        for q in range(4):
+        for h in range(4):
             for w, hbm in enumerate((wi_scales, wh_scales)):
                 nc.sync.dma_start(
-                    out=ws_raw[32 * q : 32 * q + 4, w * CH : (w + 1) * CH].bitcast(I32),
-                    in_=hbm[0, 4 * q : 4 * q + 4, :].bitcast(I32),
+                    out=ws_raw[32 * h : 32 * h + 4, w * CH : (w + 1) * CH].bitcast(I32),
+                    in_=hbm[0, 4 * h : 4 * h + 4, :].bitcast(I32),
                 )
             nc.sync.dma_start(
-                out=wts[32 * q : 32 * q + 4, :].bitcast(I32), in_=wt_scales[0, 4 * q : 4 * q + 4, :].bitcast(I32)
+                out=wts[32 * h : 32 * h + 4, :].bitcast(I32), in_=wt_scales[0, 4 * h : 4 * h + 4, :].bitcast(I32)
             )
         for g in range(2, AHEAD):
             load(g)
@@ -222,8 +217,7 @@ def tile_lstmcell_pa_t_w8_kernel(
             if s + AHEAD < GROUPS:
                 load(s + AHEAD)
             if 0 <= s - 2 < GROUPS:
-                mq[s - 2] = quant(meg[s - 2][:], "mc", "ms")
-                xq[s - 2] = quant(xg[s - 2][:], "xc", "xs")
+                quant_in(s - 2)
             if s == 2:
                 nc.vector.tensor_copy(
                     out=ws[:].rearrange("p (w t m) -> p w t m", w=2, t=PACK),

@@ -102,11 +102,13 @@ def tile_lstmcell_pa_t_w8_kernel(
                         nc.tensor.transpose(pt[:, i, u, :], words[:, base + u : base + K // 2 : 2], ident[:])
                 nc.scalar.copy(out=dst_w[:, 2 * b : 2 * b + 2], in_=pt[:].rearrange("p i u r -> p i r u"))
 
-        def transposes(g):
+        def turn_me(g):
             t = turnp.tile([P, 2 * GT * PACK], BF16, name="turned", align_bytes=64)
-            turn(me[g][:].rearrange("p i k -> p (i k)"), t[:, 0 : GT * PACK])
-            turn(xw[g][:], t[:, GT * PACK : 2 * GT * PACK])
             turned[g] = t
+            turn(me[g][:].rearrange("p i k -> p (i k)"), t[:, 0 : GT * PACK])
+
+        def turn_x(g):
+            turn(xw[g][:], turned[g][:, GT * PACK : 2 * GT * PACK])
 
         def quant_in(g):
             codes = work.tile([P, 2 * GT], U32, name="qc", align_bytes=64)
@@ -114,9 +116,12 @@ def tile_lstmcell_pa_t_w8_kernel(
             nc.vector.quantize_mx(out=codes[:].bitcast(FP8X4), scales=scales[:], in_=turned[g][:])
             q[g] = (codes, scales)
 
-        def gates(g):
-            s = work.tile([P, PACK, GT], F32, name="sig")
-            for t in range(PACK):
+        def gates(g, ts):
+            if g not in sig:
+                s = work.tile([P, PACK, GT], F32, name="sig")
+                sig[g] = s
+            s = sig[g]
+            for t in ts:
                 cols = slice(t * P, (t + 1) * P)
                 pm = pmg.tile([P, GT], F32, name="pm")
                 nc.tensor.matmul_mx(
@@ -128,7 +133,6 @@ def tile_lstmcell_pa_t_w8_kernel(
                     rhs=q[g][0][:, 0:GT].bitcast(FP8X4), rhs_scale=q[g][1][:, 0:GT], start=False, stop=True,
                 )
                 nc.scalar.activation(out=s[:, t, :], in_=pm[:], func=ACT.Sigmoid, bias=bias[:, t : t + 1])
-            sig[g] = s
 
         def pieces_of(g):
             return ((0, 2), (2, 3), (3, 4)) if g == GROUPS - 1 else ((0, G),)
@@ -207,29 +211,38 @@ def tile_lstmcell_pa_t_w8_kernel(
                 in_=ps[:].rearrange("p t n -> p n t"),
             )
         nc.scalar.copy(out=bias[:], in_=bias_bf[:])
+
         for raw, dst in ((wi_raw, wi), (wh_raw, wh)):
             nc.vector.tensor_copy(
                 out=dst[:].bitcast(I32).rearrange("p (t m) -> p t m", t=PACK),
                 in_=raw[:].bitcast(I32).rearrange("p (m t) -> p t m", t=PACK),
             )
 
+        def permute_scales():
+            nc.vector.tensor_copy(
+                out=ws[:].rearrange("p (w t m) -> p w t m", w=2, t=PACK),
+                in_=ws_raw[:].rearrange("p (w m t) -> p w t m", w=2, t=PACK),
+            )
+
         for s in range(GROUPS + 5):
             if s + AHEAD < GROUPS:
                 load(s + AHEAD)
+            if s == 2:
+                permute_scales()
+                widen(s)
             if 0 <= s - 2 < GROUPS:
                 quant_in(s - 2)
-            if s == 2:
-                nc.vector.tensor_copy(
-                    out=ws[:].rearrange("p (w t m) -> p w t m", w=2, t=PACK),
-                    in_=ws_raw[:].rearrange("p (w m t) -> p w t m", w=2, t=PACK),
-                )
             if 0 <= s - 4 < GROUPS:
                 gate(s - 4)
             if 0 <= s - 3 < GROUPS:
-                gates(s - 3)
+                gates(s - 3, (0, 1))
             if 0 <= s - 1 < GROUPS:
-                transposes(s - 1)
-            if s < GROUPS:
+                turn_me(s - 1)
+            if 0 <= s - 3 < GROUPS:
+                gates(s - 3, (2, 3))
+            if 0 <= s - 1 < GROUPS:
+                turn_x(s - 1)
+            if s < GROUPS and s != 2:
                 widen(s)
             if 0 <= s - 4 < GROUPS:
                 quant_gated(s - 4)

@@ -137,30 +137,34 @@ def tile_lstmcell_pa_t_w8_kernel(
         def pieces_of(g):
             return ((0, 2), (2, 3), (3, 4)) if g == GROUPS - 1 else ((0, G),)
 
-        def gate(g):
-            t = work.tile([P, GT * PACK], BF16, name="gated", align_bytes=64)
-            for i0, i1 in pieces_of(g):
+        def gate(g, pieces):
+            if g not in gated:
+                fresh = work.tile([P, GT * PACK], BF16, name="gated", align_bytes=64)
+                gated[g] = fresh
+            t = gated[g]
+            for i0, i1 in pieces:
                 rows = slice(i0 * P, i1 * P)
                 cols = slice(i0 * P * PACK, i1 * P * PACK)
                 nc.vector.tensor_tensor(
-                    out=t[:, cols].rearrange("p (c i t) -> p c t i", i=4, t=PACK),
-                    in0=sig[g][:, :, rows].rearrange("p t (c i) -> p c t i", i=4),
-                    in1=turned[g][:, cols].rearrange("p (c i t) -> p c t i", i=4, t=PACK),
+                    out=t[:, cols].rearrange("p (c i t) -> p c t i", i=2, t=PACK),
+                    in0=sig[g][:, :, rows].rearrange("p t (c i) -> p c t i", i=2),
+                    in1=turned[g][:, cols].rearrange("p (c i t) -> p c t i", i=2, t=PACK),
                     op=MULT,
                 )
-            gated[g] = t
 
-        def quant_gated(g):
-            codes = work.tile([P, GT], U32, name="gc", align_bytes=64)
-            scales = work.tile([P, GT], U8, name="gs", align_bytes=64)
-            for i0, i1 in pieces_of(g):
+        def quant_gated(g, pieces):
+            if g not in gq:
+                codes = work.tile([P, GT], U32, name="gc", align_bytes=64)
+                scales = work.tile([P, GT], U8, name="gs", align_bytes=64)
+                gq[g] = (codes, scales)
+            codes, scales = gq[g]
+            for i0, i1 in pieces:
                 rows = slice(i0 * P, i1 * P)
                 nc.vector.quantize_mx(
                     out=codes[:, rows].bitcast(FP8X4),
                     scales=scales[:, rows],
                     in_=gated[g][:, i0 * P * PACK : i1 * P * PACK],
                 )
-            gq[g] = (codes, scales)
 
         def read_out(g):
             o = outp.tile([P, G, N_OUT], F32, name="res")
@@ -186,21 +190,26 @@ def tile_lstmcell_pa_t_w8_kernel(
         nc.sync.dma_start(out=s_col[:], in_=x_scale.rearrange("o (p t) -> p (o t)", t=PACK))
         nc.sync.dma_start(out=wi_raw[:].bitcast(I32), in_=wi_words[0].rearrange("p n t -> p (n t)").bitcast(I32))
         nc.sync.dma_start(out=wh_raw[:].bitcast(I32), in_=wh_words[0].rearrange("p n t -> p (n t)").bitcast(I32))
-        load(0)
-        load(1)
-        nc.sync.dma_start(out=bias_bf[:], in_=mem_bias.rearrange("(p t) -> p t", t=PACK))
-        nc.sync.dma_start(out=wt[:].bitcast(I32), in_=wt_words[0].rearrange("p n t -> p (n t)").bitcast(I32))
+        load_x(0)
+        load_me(0)
+        load_x(1)
+        load_x(2)
+        load_me(1)
         for h in range(4):
             for w, hbm in enumerate((wi_scales, wh_scales)):
                 nc.sync.dma_start(
                     out=ws_raw[32 * h : 32 * h + 4, w * CH : (w + 1) * CH].bitcast(I32),
                     in_=hbm[0, 4 * h : 4 * h + 4, :].bitcast(I32),
                 )
+        nc.sync.dma_start(out=bias_bf[:], in_=mem_bias.rearrange("(p t) -> p t", t=PACK))
+        load_me(2)
+        load_x(3)
+        load_me(3)
+        nc.sync.dma_start(out=wt[:].bitcast(I32), in_=wt_words[0].rearrange("p n t -> p (n t)").bitcast(I32))
+        for h in range(4):
             nc.sync.dma_start(
                 out=wts[32 * h : 32 * h + 4, :].bitcast(I32), in_=wt_scales[0, 4 * h : 4 * h + 4, :].bitcast(I32)
             )
-        for g in range(2, AHEAD):
-            load(g)
 
         ps = ptp.tile([P, PACK, P], F32, name="pt")
         for t in range(PACK):
@@ -210,7 +219,6 @@ def tile_lstmcell_pa_t_w8_kernel(
                 out=scale[:, j * K : (j + 1) * K].rearrange("p (n t) -> p n t", t=PACK),
                 in_=ps[:].rearrange("p t n -> p n t"),
             )
-        nc.scalar.copy(out=bias[:], in_=bias_bf[:])
 
         for raw, dst in ((wi_raw, wi), (wh_raw, wh)):
             nc.vector.tensor_copy(
@@ -227,13 +235,14 @@ def tile_lstmcell_pa_t_w8_kernel(
         for s in range(GROUPS + 5):
             if s + AHEAD < GROUPS:
                 load(s + AHEAD)
-            if s == 2:
-                permute_scales()
-                widen(s)
             if 0 <= s - 2 < GROUPS:
                 quant_in(s - 2)
+            if s == 2:
+                permute_scales()
+            if s == 3:
+                nc.scalar.copy(out=bias[:], in_=bias_bf[:])
             if 0 <= s - 4 < GROUPS:
-                gate(s - 4)
+                gate(s - 4, pieces_of(s - 4)[0:2])
             if 0 <= s - 3 < GROUPS:
                 gates(s - 3, (0, 1))
             if 0 <= s - 1 < GROUPS:
@@ -242,9 +251,11 @@ def tile_lstmcell_pa_t_w8_kernel(
                 gates(s - 3, (2, 3))
             if 0 <= s - 1 < GROUPS:
                 turn_x(s - 1)
-            if s < GROUPS and s != 2:
+            if s < GROUPS:
                 widen(s)
             if 0 <= s - 4 < GROUPS:
-                quant_gated(s - 4)
+                quant_gated(s - 4, pieces_of(s - 4)[0:1])
+                gate(s - 4, pieces_of(s - 4)[2:])
+                quant_gated(s - 4, pieces_of(s - 4)[1:])
             if 0 <= s - 5 < GROUPS:
                 read_out(s - 5)

@@ -56,8 +56,8 @@ def tile_lstmcell_pa_t_w8_kernel(
         wi = keep.tile([P, CH], U32, name="wi", align_bytes=64)
         wh = keep.tile([P, CH], U32, name="wh", align_bytes=64)
         wt = keep.tile([P, N_OUT], U32, name="wt", align_bytes=64)
-        ws_raw = keep.tile([P, 2 * CH], U8, name="ws_raw", align_bytes=64)
-        ws = keep.tile([P, 2 * CH], U8, name="ws", align_bytes=64)
+        ws_raw = keep.tile([P, CH], U8, name="ws_raw", align_bytes=64)
+        ws = keep.tile([P, CH], U8, name="ws", align_bytes=64)
         wts = keep.tile([P, N_OUT], U8, name="wts", align_bytes=64)
 
         xb, me, xw, turned, q = {}, {}, {}, {}, {}
@@ -125,11 +125,11 @@ def tile_lstmcell_pa_t_w8_kernel(
                 cols = slice(t * P, (t + 1) * P)
                 pm = pmg.tile([P, GT], F32, name="pm")
                 nc.tensor.matmul_mx(
-                    out=pm[:], lhsT=wi[:, cols].bitcast(FP8X4), lhsT_scale=ws[:, t * P : (t + 1) * P],
+                    out=pm[:], lhsT=wi[:, cols].bitcast(FP8X4), lhsT_scale=ws[:, cols],
                     rhs=q[g][0][:, GT:].bitcast(FP8X4), rhs_scale=q[g][1][:, GT:], start=True, stop=False,
                 )
                 nc.tensor.matmul_mx(
-                    out=pm[:], lhsT=wh[:, cols].bitcast(FP8X4), lhsT_scale=ws[:, CH + t * P : CH + (t + 1) * P],
+                    out=pm[:], lhsT=wh[:, cols].bitcast(FP8X4), lhsT_scale=ws[4:, cols],
                     rhs=q[g][0][:, 0:GT].bitcast(FP8X4), rhs_scale=q[g][1][:, 0:GT], start=False, stop=True,
                 )
                 nc.scalar.activation(out=s[:, t, :], in_=pm[:], func=ACT.Sigmoid, bias=bias[:, t : t + 1])
@@ -146,9 +146,9 @@ def tile_lstmcell_pa_t_w8_kernel(
                 rows = slice(i0 * P, i1 * P)
                 cols = slice(i0 * P * PACK, i1 * P * PACK)
                 nc.vector.tensor_tensor(
-                    out=t[:, cols].rearrange("p (c i t) -> p c t i", i=2, t=PACK),
-                    in0=sig[g][:, :, rows].rearrange("p t (c i) -> p c t i", i=2),
-                    in1=turned[g][:, cols].rearrange("p (c i t) -> p c t i", i=2, t=PACK),
+                    out=t[:, cols].rearrange("p (c i t) -> p c t i", i=4, t=PACK),
+                    in0=sig[g][:, :, rows].rearrange("p t (c i) -> p c t i", i=4),
+                    in1=turned[g][:, cols].rearrange("p (c i t) -> p c t i", i=4, t=PACK),
                     op=MULT,
                 )
 
@@ -198,7 +198,7 @@ def tile_lstmcell_pa_t_w8_kernel(
         for h in range(4):
             for w, hbm in enumerate((wi_scales, wh_scales)):
                 nc.sync.dma_start(
-                    out=ws_raw[32 * h : 32 * h + 4, w * CH : (w + 1) * CH].bitcast(I32),
+                    out=ws_raw[32 * h + 4 * w : 32 * h + 4 * w + 4, :].bitcast(I32),
                     in_=hbm[0, 4 * h : 4 * h + 4, :].bitcast(I32),
                 )
         nc.sync.dma_start(out=bias_bf[:], in_=mem_bias.rearrange("(p t) -> p t", t=PACK))
@@ -228,8 +228,8 @@ def tile_lstmcell_pa_t_w8_kernel(
 
         def permute_scales():
             nc.vector.tensor_copy(
-                out=ws[:].rearrange("p (w t m) -> p w t m", w=2, t=PACK),
-                in_=ws_raw[:].rearrange("p (w m t) -> p w t m", w=2, t=PACK),
+                out=ws[:].rearrange("p (t m) -> p t m", t=PACK),
+                in_=ws_raw[:].rearrange("p (m t) -> p t m", t=PACK),
             )
 
         for s in range(GROUPS + 5):

from contextlib import ExitStack

import concourse.mybir as mybir
from concourse.masks import make_identity

TOKENS, K, CH, N_OUT = 8192, 512, 512, 256
FLOPS = 2 * TOKENS * (K * CH + CH * CH + CH * N_OUT)

F32 = mybir.dt.float32
BF16 = mybir.dt.bfloat16
I32 = mybir.dt.int32
U32 = mybir.dt.uint32
U8 = mybir.dt.uint8
FP8 = mybir.dt.float8_e4m3fn
FP8X4 = mybir.dt.float8_e4m3fn_x4
MULT = mybir.AluOpType.mult
ACT = mybir.ActivationFunctionType

P = 128
PACK = 4
TILES = TOKENS // P
G = 4
GROUPS = TILES // G
GT = G * P
AHEAD = 4


def tile_lstmcell_pa_t_w8_kernel(
    tc, x_bytes, x_scale, me_output, wi_words, wi_scales, wh_words, wh_scales, wt_words, wt_scales, mem_bias, out
):
    nc = tc.nc
    x_hbm = x_bytes.rearrange("(p i) k -> p i k", i=TILES)
    me_hbm = me_output.rearrange("(p i) k -> p i k", i=TILES)
    out_hbm = out.rearrange("(p i) n -> p i n", i=TILES)

    with ExitStack() as ctx:
        keep = ctx.enter_context(tc.tile_pool(name="keep", bufs=1))
        xin = ctx.enter_context(tc.tile_pool(name="xin", bufs=6))
        mein = ctx.enter_context(tc.tile_pool(name="mein", bufs=7))
        work = ctx.enter_context(tc.tile_pool(name="work", bufs=3))
        turnp = ctx.enter_context(tc.tile_pool(name="turnp", bufs=5))
        outp = ctx.enter_context(tc.tile_pool(name="outp", bufs=3))
        ptp = ctx.enter_context(tc.psum_pool(name="ptp", bufs=3))
        pmg = ctx.enter_context(tc.psum_pool(name="pmg", bufs=3))
        pout = ctx.enter_context(tc.psum_pool(name="pout", bufs=2))
        ctx.enter_context(tc.manual_schedule())

        ident = keep.tile([P, P], F32, name="ident")
        s_col = keep.tile([P, PACK], F32, name="s_col")
        scale = keep.tile([P, G * K], F32, name="scale")
        bias_bf = keep.tile([P, PACK], BF16, name="bias_bf")
        bias = keep.tile([P, PACK], F32, name="bias")
        warm = keep.tile([P, 1], F32, name="warm")
        wi_raw = keep.tile([P, CH], U32, name="wi_raw", align_bytes=64)
        wh_raw = keep.tile([P, CH], U32, name="wh_raw", align_bytes=64)
        wi = keep.tile([P, CH], U32, name="wi", align_bytes=64)
        wh = keep.tile([P, CH], U32, name="wh", align_bytes=64)
        wt = keep.tile([P, N_OUT], U32, name="wt", align_bytes=64)
        ws_raw = keep.tile([P, CH], U8, name="ws_raw", align_bytes=64)
        ws = keep.tile([P, CH], U8, name="ws", align_bytes=64)
        wts = keep.tile([P, N_OUT], U8, name="wts", align_bytes=64)

        xb, me, xw, turned, q = {}, {}, {}, {}, {}
        sig, gated, gq = {}, {}, {}

        def load_x(g):
            t = xin.tile([P, G, K], U8, name="xb")
            nc.sync.dma_start(out=t[:], in_=x_hbm[:, g * G : (g + 1) * G, :])
            xb[g] = t

        def load_me(g):
            t = mein.tile([P, G, K], BF16, name="me")
            nc.sync.dma_start(out=t[:], in_=me_hbm[:, g * G : (g + 1) * G, :])
            me[g] = t

        def load(g):
            load_x(g)
            load_me(g)

        def widen(g):
            t = work.tile([P, G * K], BF16, name="xw")
            src = xb[g][:].rearrange("p i k -> p (i k)")
            pieces = G if g == 0 else 1
            w = G * K // pieces
            for j in range(pieces):
                nc.vector.tensor_tensor(
                    out=t[:, j * w : (j + 1) * w],
                    in0=src[:, j * w : (j + 1) * w].bitcast(FP8),
                    in1=scale[:, 0:w],
                    op=MULT,
                )
            xw[g] = t

        def turn(src, dst):
            words = src.bitcast(F32)
            dst_w = dst.bitcast(F32).rearrange("p (i r u) -> p i r u", i=G, u=2)
            for b in range(G // 2):
                pt = ptp.tile([P, 2, 2, P], F32, name="pt")
                for i in range(2):
                    for u in range(2):
                        base = (2 * b + i) * (K // 2)
                        nc.tensor.transpose(pt[:, i, u, :], words[:, base + u : base + K // 2 : 2], ident[:])
                nc.scalar.copy(out=dst_w[:, 2 * b : 2 * b + 2], in_=pt[:].rearrange("p i u r -> p i r u"))

        def turn_me(g):
            t = turnp.tile([P, 2 * GT * PACK], BF16, name="turned", align_bytes=64)
            turned[g] = t
            turn(me[g][:].rearrange("p i k -> p (i k)"), t[:, 0 : GT * PACK])

        def turn_x(g):
            turn(xw[g][:], turned[g][:, GT * PACK : 2 * GT * PACK])

        def quant_in(g):
            codes = work.tile([P, 2 * GT], U32, name="qc", align_bytes=64)
            scales = work.tile([P, 2 * GT], U8, name="qs", align_bytes=64)
            nc.vector.quantize_mx(out=codes[:].bitcast(FP8X4), scales=scales[:], in_=turned[g][:])
            q[g] = (codes, scales)

        def gates(g, ts):
            if g not in sig:
                s = work.tile([P, PACK, GT], F32, name="sig")
                sig[g] = s
            s = sig[g]
            for t in ts:
                cols = slice(t * P, (t + 1) * P)
                pm = pmg.tile([P, GT], F32, name="pm")
                nc.tensor.matmul_mx(
                    out=pm[:], lhsT=wi[:, cols].bitcast(FP8X4), lhsT_scale=ws[:, cols],
                    rhs=q[g][0][:, GT:].bitcast(FP8X4), rhs_scale=q[g][1][:, GT:], start=True, stop=False,
                )
                nc.tensor.matmul_mx(
                    out=pm[:], lhsT=wh[:, cols].bitcast(FP8X4), lhsT_scale=ws[4:, cols],
                    rhs=q[g][0][:, 0:GT].bitcast(FP8X4), rhs_scale=q[g][1][:, 0:GT], start=False, stop=True,
                )
                nc.scalar.activation(out=s[:, t, :], in_=pm[:], func=ACT.Sigmoid, bias=bias[:, t : t + 1])

        def pieces_of(g):
            return ((0, 2), (2, 3), (3, 4)) if g == GROUPS - 1 else ((0, G),)

        def gate(g, pieces):
            if g not in gated:
                fresh = work.tile([P, GT * PACK], BF16, name="gated", align_bytes=64)
                gated[g] = fresh
            t = gated[g]
            for i0, i1 in pieces:
                rows = slice(i0 * P, i1 * P)
                cols = slice(i0 * P * PACK, i1 * P * PACK)
                nc.vector.tensor_tensor(
                    out=t[:, cols].rearrange("p (c i t) -> p c t i", i=4, t=PACK),
                    in0=sig[g][:, :, rows].rearrange("p t (c i) -> p c t i", i=4),
                    in1=turned[g][:, cols].rearrange("p (c i t) -> p c t i", i=4, t=PACK),
                    op=MULT,
                )

        def quant_gated(g, pieces):
            if g not in gq:
                codes = work.tile([P, GT], U32, name="gc", align_bytes=64)
                scales = work.tile([P, GT], U8, name="gs", align_bytes=64)
                gq[g] = (codes, scales)
            codes, scales = gq[g]
            for i0, i1 in pieces:
                rows = slice(i0 * P, i1 * P)
                nc.vector.quantize_mx(
                    out=codes[:, rows].bitcast(FP8X4),
                    scales=scales[:, rows],
                    in_=gated[g][:, i0 * P * PACK : i1 * P * PACK],
                )

        def read_out(g):
            o = outp.tile([P, G, N_OUT], F32, name="res")
            for i0, i1 in pieces_of(g):
                for b in range(i0, i1, 2):
                    e = min(b + 2, i1)
                    po = pout.tile([P, 2, N_OUT], F32, name="po")
                    for i in range(b, e):
                        cols = slice(i * P, (i + 1) * P)
                        nc.tensor.matmul_mx(
                            out=po[:, i - b, :], lhsT=gq[g][0][:, cols].bitcast(FP8X4), lhsT_scale=gq[g][1][:, cols],
                            rhs=wt[:].bitcast(FP8X4), rhs_scale=wts[:], start=True, stop=True,
                        )
                    nc.scalar.copy(out=o[:, b:e, :], in_=po[:, 0 : e - b, :])
                nc.sync.dma_start(out=out_hbm[:, g * G + i0 : g * G + i1, :], in_=o[:, i0:i1, :])

        make_identity(nc, ident[:])
        nc.gpsimd.memset(ws_raw[:].bitcast(I32), 0)
        nc.gpsimd.memset(wts[:].bitcast(I32), 0)
        nc.gpsimd.memset(warm[:], 0.0)
        nc.scalar.activation(out=warm[:], in_=warm[:], func=ACT.Sigmoid)

        nc.sync.dma_start(out=s_col[:], in_=x_scale.rearrange("o (p t) -> p (o t)", t=PACK))
        nc.sync.dma_start(out=wi_raw[:].bitcast(I32), in_=wi_words[0].rearrange("p n t -> p (n t)").bitcast(I32))
        nc.sync.dma_start(out=wh_raw[:].bitcast(I32), in_=wh_words[0].rearrange("p n t -> p (n t)").bitcast(I32))
        load_x(0)
        load_me(0)
        load_x(1)
        load_x(2)
        load_me(1)
        for h in range(4):
            for w, hbm in enumerate((wi_scales, wh_scales)):
                nc.sync.dma_start(
                    out=ws_raw[32 * h + 4 * w : 32 * h + 4 * w + 4, :].bitcast(I32),
                    in_=hbm[0, 4 * h : 4 * h + 4, :].bitcast(I32),
                )
        nc.sync.dma_start(out=bias_bf[:], in_=mem_bias.rearrange("(p t) -> p t", t=PACK))
        load_me(2)
        load_x(3)
        load_me(3)
        nc.sync.dma_start(out=wt[:].bitcast(I32), in_=wt_words[0].rearrange("p n t -> p (n t)").bitcast(I32))
        for h in range(4):
            nc.sync.dma_start(
                out=wts[32 * h : 32 * h + 4, :].bitcast(I32), in_=wt_scales[0, 4 * h : 4 * h + 4, :].bitcast(I32)
            )

        ps = ptp.tile([P, PACK, P], F32, name="pt")
        for t in range(PACK):
            nc.tensor.transpose(ps[:, t, :], s_col[:, t : t + 1].to_broadcast([P, P]), ident[:])
        for j in range(G):
            nc.scalar.copy(
                out=scale[:, j * K : (j + 1) * K].rearrange("p (n t) -> p n t", t=PACK),
                in_=ps[:].rearrange("p t n -> p n t"),
            )

        for raw, dst in ((wi_raw, wi), (wh_raw, wh)):
            nc.vector.tensor_copy(
                out=dst[:].bitcast(I32).rearrange("p (t m) -> p t m", t=PACK),
                in_=raw[:].bitcast(I32).rearrange("p (m t) -> p t m", t=PACK),
            )

        def permute_scales():
            nc.vector.tensor_copy(
                out=ws[:].rearrange("p (t m) -> p t m", t=PACK),
                in_=ws_raw[:].rearrange("p (m t) -> p t m", t=PACK),
            )

        for s in range(GROUPS + 5):
            if s + AHEAD < GROUPS:
                load(s + AHEAD)
            if 0 <= s - 2 < GROUPS:
                quant_in(s - 2)
            if s == 2:
                permute_scales()
            if s == 3:
                nc.scalar.copy(out=bias[:], in_=bias_bf[:])
            if 0 <= s - 4 < GROUPS:
                gate(s - 4, pieces_of(s - 4)[0:2])
            if 0 <= s - 3 < GROUPS:
                gates(s - 3, (0, 1))
            if 0 <= s - 1 < GROUPS:
                turn_me(s - 1)
            if 0 <= s - 3 < GROUPS:
                gates(s - 3, (2, 3))
            if 0 <= s - 1 < GROUPS:
                turn_x(s - 1)
            if s < GROUPS:
                widen(s)
            if 0 <= s - 4 < GROUPS:
                quant_gated(s - 4, pieces_of(s - 4)[0:1])
                gate(s - 4, pieces_of(s - 4)[2:])
                quant_gated(s - 4, pieces_of(s - 4)[1:])
            if 0 <= s - 5 < GROUPS:
                read_out(s - 5)
